import numpy as np
import ml_dtypes

BF16 = ml_dtypes.bfloat16


def bf(x):
    return np.asarray(x, np.float32).astype(BF16)


def f32(x):
    return np.asarray(x, np.float32)


def f64(x):
    return np.asarray(x).astype(np.float64)


def striped(idx):
    return np.tile(idx.reshape(-1, 16).T, (8, 1))


H, D, NE, HN, CD, C, S, N = 8, 128, 64, 32, 512, 1024, 256, 128


def setup_inputs():
    theta = 2.0 * np.pi * np.random.random_sample((HN, N))
    return {"base": f32(np.random.standard_normal((C, S))), "y": bf(np.random.standard_normal((CD, N))), "wk": bf(np.random.standard_normal((CD, C)) / np.sqrt(CD)), "rope_cos": f32(np.cos(theta)), "rope_sin": f32(np.sin(theta)), "offs": striped(np.random.permutation(S)[:N])}


def reference(base, y, wk, rope_cos, rope_sin, offs):
    idx = offs[:16].T.reshape(-1)
    k = (f64(wk).T @ f64(y)).reshape(H, D, N)
    cos = f64(rope_cos)[None]
    sin = f64(rope_sin)[None]
    u1 = k[:, :HN]
    u2 = k[:, HN:NE]
    a = np.concatenate([u1 * cos, u2 * cos, k[:, NE:]], axis=1)
    b = np.concatenate([(-u2) * sin, u1 * sin, np.zeros((H, D - NE, N))], axis=1)
    res = f64(base).copy()
    res[:, idx] = (a + b).reshape(C, N)
    return res

@@ -1,0 +1,73 @@
+import concourse.mybir as mybir
+
+FLOPS = 2 * 512 * 1024 * 128
+
+P = 128
+HEADS = 8
+TOKENS = 128
+SLOTS = 256
+KB = 4
+HALF = 32
+
+BF16, F32, U16 = mybir.dt.bfloat16, mybir.dt.float32, mybir.dt.uint16
+MULT, ADD = mybir.AluOpType.mult, mybir.AluOpType.add
+
+
+def tile_crossattention_s_kernel(tc, base, y, wk, rope_cos, rope_sin, offs, out):
+    nc = tc.nc
+    with (
+        tc.tile_pool(name="held", bufs=1) as held,
+        tc.tile_pool(name="work", bufs=3) as work,
+        tc.psum_pool(name="psum_k", bufs=4) as psum_k,
+        tc.psum_pool(name="psum_partner", bufs=4) as psum_partner,
+    ):
+        offsets = held.tile([P, TOKENS // 16], U16, name="offsets")
+        nc.sync.dma_start(offsets[:], offs)
+
+        y_sb = held.tile([P, KB, TOKENS], BF16, name="y_sb")
+        nc.sync.dma_start(y_sb[:], y.rearrange("(p kb) j -> p kb j", kb=KB))
+        wk_view = wk.rearrange("(p kb) c -> p kb c", kb=KB)
+        wk_sb = []
+        for pair in range(HEADS // 2):
+            wk_pair = held.tile([P, KB, 2 * P], BF16, name=f"wk_pair{pair}")
+            nc.sync.dma_start(wk_pair[:], wk_view[:, :, pair * 2 * P : (pair + 1) * 2 * P])
+            wk_sb.append(wk_pair)
+
+        cos_t = held.tile([P, TOKENS], F32, name="cos_t")
+        nc.scalar.dma_start(cos_t[0:HALF, :], rope_cos)
+        nc.scalar.dma_start(cos_t[HALF : 2 * HALF, :], rope_cos)
+        nc.gpsimd.memset(cos_t[2 * HALF : P, :], 1.0)
+        sin_t = held.tile([2 * HALF, TOKENS], F32, name="sin_t")
+        nc.scalar.dma_start(sin_t[0:HALF, :], rope_sin)
+        nc.scalar.dma_start(sin_t[HALF : 2 * HALF, :], rope_sin)
+        nc.scalar.mul(sin_t[0:HALF, :], sin_t[0:HALF, :], -1.0)
+
+        windows = []
+        for h in range(HEADS):
+            window = held.tile([P, SLOTS], F32, name=f"window{h}")
+            nc.scalar.dma_start(window[:], base[h * P : (h + 1) * P, :])
+            windows.append(window)
+
+        b_all = held.tile([P, HEADS, TOKENS], F32, name="b_all")
+        nc.gpsimd.memset(b_all[2 * HALF : P, :, :], 0.0)
+
+        for h in range(HEADS):
+            wk_pair = wk_sb[h // 2]
+            c0 = (h % 2) * P
+            k_ps = psum_k.tile([P, TOKENS], F32, name="k_ps")
+            for kb in range(KB):
+                nc.tensor.matmul(k_ps[:], wk_pair[:, kb, c0 : c0 + P], y_sb[:, kb, :],
+                                 start=(kb == 0), stop=(kb == KB - 1))
+            partner_ps = psum_partner.tile([P, TOKENS], F32, name="partner_ps")
+            for kb in range(KB):
+                nc.tensor.matmul(partner_ps[0:HALF, :], wk_pair[:, kb, c0 + HALF : c0 + 2 * HALF],
+                                 y_sb[:, kb, :], start=(kb == 0), stop=(kb == KB - 1))
+            for kb in range(KB):
+                nc.tensor.matmul(partner_ps[HALF : 2 * HALF, :], wk_pair[:, kb, c0 : c0 + HALF],
+                                 y_sb[:, kb, :], start=(kb == 0), stop=(kb == KB - 1))
+
+            a = work.tile([P, TOKENS], F32, name="a")
+            nc.vector.tensor_tensor(a[:], k_ps[:], cos_t[:], MULT)
+            nc.vector.tensor_tensor(b_all[0 : 2 * HALF, h, :], partner_ps[0 : 2 * HALF, :], sin_t[:], MULT)
+            nc.vector.tensor_tensor(windows[h][:].indirect(offsets[:]), a[:], b_all[:, h, :], ADD)
+            nc.sync.dma_start(out[h * P : (h + 1) * P, :], windows[h][:])

@@ -8,6 +8,7 @@ TOKENS = 128
 SLOTS = 256
 KB = 4
 HALF = 32
+WARMUP = 4
 
 BF16, F32, U16 = mybir.dt.bfloat16, mybir.dt.float32, mybir.dt.uint16
 MULT, ADD = mybir.AluOpType.mult, mybir.AluOpType.add
@@ -18,36 +19,46 @@ def tile_crossattention_s_kernel(tc, base, y, wk, rope_cos, rope_sin, offs, out)
     with (
         tc.tile_pool(name="held", bufs=1) as held,
         tc.tile_pool(name="work", bufs=3) as work,
-        tc.psum_pool(name="psum_k", bufs=4) as psum_k,
-        tc.psum_pool(name="psum_partner", bufs=4) as psum_partner,
+        tc.psum_pool(name="psum_warm", bufs=1) as psum_warm,
+        tc.psum_pool(name="psum_k", bufs=3) as psum_k,
+        tc.psum_pool(name="psum_partner", bufs=3) as psum_partner,
     ):
+        zeros_bf = held.tile([P, 512], BF16, name="zeros_bf")
+        nc.vector.memset(zeros_bf[:], 0.0)
+        warm_ps = psum_warm.tile([P, 512], F32, name="warm_ps")
+        for i in range(WARMUP):
+            nc.tensor.matmul(warm_ps[:], zeros_bf[:, 0:P], zeros_bf[:], start=True, stop=True)
+
         offsets = held.tile([P, TOKENS // 16], U16, name="offsets")
-        nc.sync.dma_start(offsets[:], offs)
-
         y_sb = held.tile([P, KB, TOKENS], BF16, name="y_sb")
-        nc.sync.dma_start(y_sb[:], y.rearrange("(p kb) j -> p kb j", kb=KB))
+        wk_sb = [held.tile([P, KB, 2 * P], BF16, name=f"wk_pair{pair}") for pair in range(HEADS // 2)]
         wk_view = wk.rearrange("(p kb) c -> p kb c", kb=KB)
-        wk_sb = []
-        for pair in range(HEADS // 2):
-            wk_pair = held.tile([P, KB, 2 * P], BF16, name=f"wk_pair{pair}")
-            nc.sync.dma_start(wk_pair[:], wk_view[:, :, pair * 2 * P : (pair + 1) * 2 * P])
-            wk_sb.append(wk_pair)
-
         cos_t = held.tile([P, TOKENS], F32, name="cos_t")
-        nc.scalar.dma_start(cos_t[0:HALF, :], rope_cos)
-        nc.scalar.dma_start(cos_t[HALF : 2 * HALF, :], rope_cos)
-        nc.gpsimd.memset(cos_t[2 * HALF : P, :], 1.0)
         sin_t = held.tile([2 * HALF, TOKENS], F32, name="sin_t")
-        nc.scalar.dma_start(sin_t[0:HALF, :], rope_sin)
+        windows = [held.tile([P, SLOTS], F32, name=f"window{h}") for h in range(HEADS)]
+
+        def load_wk(queue, pair):
+            queue.dma_start(wk_sb[pair][:], wk_view[:, :, pair * 2 * P : (pair + 1) * 2 * P])
+
+        def load_window(queue, h):
+            queue.dma_start(windows[h][:], base[h * P : (h + 1) * P, :])
+
+        nc.sync.dma_start(y_sb[:], y.rearrange("(p kb) j -> p kb j", kb=KB))
+        load_wk(nc.scalar, 0)
+        nc.sync.dma_start(sin_t[0:HALF, :], rope_sin)
         nc.scalar.dma_start(sin_t[HALF : 2 * HALF, :], rope_sin)
-        nc.scalar.mul(sin_t[0:HALF, :], sin_t[0:HALF, :], -1.0)
+        nc.sync.dma_start(cos_t[0:HALF, :], rope_cos)
+        nc.scalar.dma_start(cos_t[HALF : 2 * HALF, :], rope_cos)
+        nc.sync.dma_start(offsets[:], offs)
+        load_window(nc.scalar, 0)
+        for pair in range(1, HEADS // 2):
+            load_wk(nc.sync, pair)
+            load_window(nc.scalar, pair)
+        for h in range(HEADS // 2, HEADS):
+            load_window(nc.sync if h % 2 == 0 else nc.scalar, h)
 
-        windows = []
-        for h in range(HEADS):
-            window = held.tile([P, SLOTS], F32, name=f"window{h}")
-            nc.scalar.dma_start(window[:], base[h * P : (h + 1) * P, :])
-            windows.append(window)
-
+        nc.vector.tensor_scalar_mul(sin_t[0:HALF, :], sin_t[0:HALF, :], -1.0)
+        nc.gpsimd.memset(cos_t[2 * HALF : P, :], 1.0)
         b_all = held.tile([P, HEADS, TOKENS], F32, name="b_all")
         nc.gpsimd.memset(b_all[2 * HALF : P, :, :], 0.0)
 
@@ -62,7 +73,6 @@ def tile_crossattention_s_kernel(tc, base, y, wk, rope_cos, rope_sin, offs, out)
             for kb in range(KB):
                 nc.tensor.matmul(partner_ps[0:HALF, :], wk_pair[:, kb, c0 + HALF : c0 + 2 * HALF],
                                  y_sb[:, kb, :], start=(kb == 0), stop=(kb == KB - 1))
-            for kb in range(KB):
                 nc.tensor.matmul(partner_ps[HALF : 2 * HALF, :], wk_pair[:, kb, c0 : c0 + HALF],
                                  y_sb[:, kb, :], start=(kb == 0), stop=(kb == KB - 1))
 
@@ -70,4 +80,4 @@ def tile_crossattention_s_kernel(tc, base, y, wk, rope_cos, rope_sin, offs, out)
             nc.vector.tensor_tensor(a[:], k_ps[:], cos_t[:], MULT)
             nc.vector.tensor_tensor(b_all[0 : 2 * HALF, h, :], partner_ps[0 : 2 * HALF, :], sin_t[:], MULT)
             nc.vector.tensor_tensor(windows[h][:].indirect(offsets[:]), a[:], b_all[:, h, :], ADD)
-            nc.sync.dma_start(out[h * P : (h + 1) * P, :], windows[h][:])
+            (nc.sync if h % 2 == 0 else nc.scalar).dma_start(out[h * P : (h + 1) * P, :], windows[h][:])

@@ -8,7 +8,7 @@ TOKENS = 128
 SLOTS = 256
 KB = 4
 HALF = 32
-WARMUP = 4
+GROUPS = ((0,), (1,), (2, 3), (4, 5), (6, 7))
 
 BF16, F32, U16 = mybir.dt.bfloat16, mybir.dt.float32, mybir.dt.uint16
 MULT, ADD = mybir.AluOpType.mult, mybir.AluOpType.add
@@ -18,23 +18,20 @@ def tile_crossattention_s_kernel(tc, base, y, wk, rope_cos, rope_sin, offs, out)
     nc = tc.nc
     with (
         tc.tile_pool(name="held", bufs=1) as held,
-        tc.tile_pool(name="work", bufs=3) as work,
-        tc.psum_pool(name="psum_warm", bufs=1) as psum_warm,
-        tc.psum_pool(name="psum_k", bufs=3) as psum_k,
-        tc.psum_pool(name="psum_partner", bufs=3) as psum_partner,
+        tc.psum_pool(name="psum", bufs=1) as psum,
     ):
-        zeros_bf = held.tile([P, 512], BF16, name="zeros_bf")
+        zeros_bf = held.tile([P, 4 * TOKENS], BF16, name="zeros_bf")
         nc.vector.memset(zeros_bf[:], 0.0)
-        warm_ps = psum_warm.tile([P, 512], F32, name="warm_ps")
-        for i in range(WARMUP):
-            nc.tensor.matmul(warm_ps[:], zeros_bf[:, 0:P], zeros_bf[:], start=True, stop=True)
+        banks = [psum.tile([P, 2, len(heads), TOKENS], F32, name=f"bank{g}") for g, heads in enumerate(GROUPS)]
+        for bank, heads in zip(banks, GROUPS):
+            nc.tensor.matmul(bank[:].rearrange("p s i j -> p (s i j)"), zeros_bf[:, 0:P],
+                             zeros_bf[:, 0 : 2 * len(heads) * TOKENS], start=True, stop=True)
 
         offsets = held.tile([P, TOKENS // 16], U16, name="offsets")
         y_sb = held.tile([P, KB, TOKENS], BF16, name="y_sb")
         wk_sb = [held.tile([P, KB, 2 * P], BF16, name=f"wk_pair{pair}") for pair in range(HEADS // 2)]
         wk_view = wk.rearrange("(p kb) c -> p kb c", kb=KB)
-        cos_t = held.tile([P, TOKENS], F32, name="cos_t")
-        sin_t = held.tile([2 * HALF, TOKENS], F32, name="sin_t")
+        table = held.tile([P, 2, TOKENS], F32, name="table")
         windows = [held.tile([P, SLOTS], F32, name=f"window{h}") for h in range(HEADS)]
 
         def load_wk(queue, pair):
@@ -45,10 +42,10 @@ def tile_crossattention_s_kernel(tc, base, y, wk, rope_cos, rope_sin, offs, out)
 
         nc.sync.dma_start(y_sb[:], y.rearrange("(p kb) j -> p kb j", kb=KB))
         load_wk(nc.scalar, 0)
-        nc.sync.dma_start(sin_t[0:HALF, :], rope_sin)
-        nc.scalar.dma_start(sin_t[HALF : 2 * HALF, :], rope_sin)
-        nc.sync.dma_start(cos_t[0:HALF, :], rope_cos)
-        nc.scalar.dma_start(cos_t[HALF : 2 * HALF, :], rope_cos)
+        nc.sync.dma_start(table[0:HALF, 1, :], rope_sin)
+        nc.scalar.dma_start(table[HALF : 2 * HALF, 1, :], rope_sin)
+        nc.sync.dma_start(table[0:HALF, 0, :], rope_cos)
+        nc.scalar.dma_start(table[HALF : 2 * HALF, 0, :], rope_cos)
         nc.sync.dma_start(offsets[:], offs)
         load_window(nc.scalar, 0)
         for pair in range(1, HEADS // 2):
@@ -57,27 +54,26 @@ def tile_crossattention_s_kernel(tc, base, y, wk, rope_cos, rope_sin, offs, out)
         for h in range(HEADS // 2, HEADS):
             load_window(nc.sync if h % 2 == 0 else nc.scalar, h)
 
-        nc.vector.tensor_scalar_mul(sin_t[0:HALF, :], sin_t[0:HALF, :], -1.0)
-        nc.gpsimd.memset(cos_t[2 * HALF : P, :], 1.0)
-        b_all = held.tile([P, HEADS, TOKENS], F32, name="b_all")
-        nc.gpsimd.memset(b_all[2 * HALF : P, :, :], 0.0)
+        nc.vector.tensor_scalar_mul(table[0:HALF, 1, :], table[0:HALF, 1, :], -1.0)
+        nc.gpsimd.memset(table[2 * HALF : P, 0, :], 1.0)
+        nc.gpsimd.memset(table[2 * HALF : P, 1, :], 0.0)
 
-        for h in range(HEADS):
-            wk_pair = wk_sb[h // 2]
-            c0 = (h % 2) * P
-            k_ps = psum_k.tile([P, TOKENS], F32, name="k_ps")
-            for kb in range(KB):
-                nc.tensor.matmul(k_ps[:], wk_pair[:, kb, c0 : c0 + P], y_sb[:, kb, :],
-                                 start=(kb == 0), stop=(kb == KB - 1))
-            partner_ps = psum_partner.tile([P, TOKENS], F32, name="partner_ps")
-            for kb in range(KB):
-                nc.tensor.matmul(partner_ps[0:HALF, :], wk_pair[:, kb, c0 + HALF : c0 + 2 * HALF],
-                                 y_sb[:, kb, :], start=(kb == 0), stop=(kb == KB - 1))
-                nc.tensor.matmul(partner_ps[HALF : 2 * HALF, :], wk_pair[:, kb, c0 : c0 + HALF],
-                                 y_sb[:, kb, :], start=(kb == 0), stop=(kb == KB - 1))
+        for g, heads in enumerate(GROUPS):
+            bank = banks[g]
+            for i, h in enumerate(heads):
+                wk_pair = wk_sb[h // 2]
+                c0 = (h % 2) * P
+                for kb in range(KB):
+                    nc.tensor.matmul(bank[:, 0, i, :], wk_pair[:, kb, c0 : c0 + P], y_sb[:, kb, :],
+                                     start=(kb == 0), stop=(kb == KB - 1))
+                for kb in range(KB):
+                    nc.tensor.matmul(bank[0:HALF, 1, i, :], wk_pair[:, kb, c0 + HALF : c0 + 2 * HALF],
+                                     y_sb[:, kb, :], start=(kb == 0), stop=(kb == KB - 1))
+                    nc.tensor.matmul(bank[HALF : 2 * HALF, 1, i, :], wk_pair[:, kb, c0 : c0 + HALF],
+                                     y_sb[:, kb, :], start=(kb == 0), stop=(kb == KB - 1))
 
-            a = work.tile([P, TOKENS], F32, name="a")
-            nc.vector.tensor_tensor(a[:], k_ps[:], cos_t[:], MULT)
-            nc.vector.tensor_tensor(b_all[0 : 2 * HALF, h, :], partner_ps[0 : 2 * HALF, :], sin_t[:], MULT)
-            nc.vector.tensor_tensor(windows[h][:].indirect(offsets[:]), a[:], b_all[:, h, :], ADD)
-            (nc.sync if h % 2 == 0 else nc.scalar).dma_start(out[h * P : (h + 1) * P, :], windows[h][:])
+            ab = held.tile([P, 2, len(heads), TOKENS], F32, name=f"ab{g}")
+            nc.vector.tensor_tensor(ab[:], bank[:], table[:].unsqueeze(2).to_broadcast([P, 2, len(heads), TOKENS]), MULT)
+            for i, h in enumerate(heads):
+                nc.vector.tensor_tensor(windows[h][:].indirect(offsets[:]), ab[:, 0, i, :], ab[:, 1, i, :], ADD)
+                (nc.sync if h % 2 == 0 else nc.scalar).dma_start(out[h * P : (h + 1) * P, :], windows[h][:])

@@ -9,6 +9,7 @@ SLOTS = 256
 KB = 4
 HALF = 32
 GROUPS = ((0,), (1,), (2, 3), (4, 5), (6, 7))
+SOFT_WINDOWS = 3
 
 BF16, F32, U16 = mybir.dt.bfloat16, mybir.dt.float32, mybir.dt.uint16
 MULT, ADD = mybir.AluOpType.mult, mybir.AluOpType.add
@@ -47,16 +48,20 @@ def tile_crossattention_s_kernel(tc, base, y, wk, rope_cos, rope_sin, offs, out)
         nc.sync.dma_start(table[0:HALF, 0, :], rope_cos)
         nc.scalar.dma_start(table[HALF : 2 * HALF, 0, :], rope_cos)
         nc.sync.dma_start(offsets[:], offs)
-        load_window(nc.scalar, 0)
-        for pair in range(1, HEADS // 2):
-            load_wk(nc.sync, pair)
-            load_window(nc.scalar, pair)
-        for h in range(HEADS // 2, HEADS):
-            load_window(nc.sync if h % 2 == 0 else nc.scalar, h)
+        load_wk(nc.scalar, 1)
+        for h in range(SOFT_WINDOWS):
+            load_window(nc.gpsimd, h)
+        load_window(nc.sync, 3)
+        load_wk(nc.scalar, 2)
+        load_window(nc.sync, 4)
+        load_wk(nc.scalar, 3)
+        load_window(nc.sync, 5)
+        load_window(nc.scalar, 6)
+        load_window(nc.sync, 7)
 
+        nc.vector.memset(table[2 * HALF : P, 0, :], 1.0)
+        nc.vector.memset(table[2 * HALF : P, 1, :], 0.0)
         nc.vector.tensor_scalar_mul(table[0:HALF, 1, :], table[0:HALF, 1, :], -1.0)
-        nc.gpsimd.memset(table[2 * HALF : P, 0, :], 1.0)
-        nc.gpsimd.memset(table[2 * HALF : P, 1, :], 0.0)
 
         for g, heads in enumerate(GROUPS):
             bank = banks[g]

@@ -8,8 +8,7 @@ TOKENS = 128
 SLOTS = 256
 KB = 4
 HALF = 32
-GROUPS = ((0,), (1,), (2, 3), (4, 5), (6, 7))
-SOFT_WINDOWS = 3
+GROUPS = ((0,), (1,), (2, 3), (4, 5), (6,), (7,))
 
 BF16, F32, U16 = mybir.dt.bfloat16, mybir.dt.float32, mybir.dt.uint16
 MULT, ADD = mybir.AluOpType.mult, mybir.AluOpType.add
@@ -48,20 +47,16 @@ def tile_crossattention_s_kernel(tc, base, y, wk, rope_cos, rope_sin, offs, out)
         nc.sync.dma_start(table[0:HALF, 0, :], rope_cos)
         nc.scalar.dma_start(table[HALF : 2 * HALF, 0, :], rope_cos)
         nc.sync.dma_start(offsets[:], offs)
-        load_wk(nc.scalar, 1)
-        for h in range(SOFT_WINDOWS):
-            load_window(nc.gpsimd, h)
-        load_window(nc.sync, 3)
-        load_wk(nc.scalar, 2)
-        load_window(nc.sync, 4)
-        load_wk(nc.scalar, 3)
-        load_window(nc.sync, 5)
-        load_window(nc.scalar, 6)
-        load_window(nc.sync, 7)
+        load_window(nc.scalar, 0)
+        for pair in range(1, HEADS // 2):
+            load_wk(nc.sync, pair)
+            load_window(nc.scalar, pair)
+        for h in range(HEADS // 2, HEADS):
+            load_window(nc.sync if h % 2 == 0 else nc.scalar, h)
 
-        nc.vector.memset(table[2 * HALF : P, 0, :], 1.0)
-        nc.vector.memset(table[2 * HALF : P, 1, :], 0.0)
         nc.vector.tensor_scalar_mul(table[0:HALF, 1, :], table[0:HALF, 1, :], -1.0)
+        nc.gpsimd.memset(table[2 * HALF : P, 0, :], 1.0)
+        nc.gpsimd.memset(table[2 * HALF : P, 1, :], 0.0)
 
         for g, heads in enumerate(GROUPS):
             bank = banks[g]

@@ -20,12 +20,10 @@ def tile_crossattention_s_kernel(tc, base, y, wk, rope_cos, rope_sin, offs, out)
         tc.tile_pool(name="held", bufs=1) as held,
         tc.psum_pool(name="psum", bufs=1) as psum,
     ):
-        zeros_bf = held.tile([P, 4 * TOKENS], BF16, name="zeros_bf")
-        nc.vector.memset(zeros_bf[:], 0.0)
         banks = [psum.tile([P, 2, len(heads), TOKENS], F32, name=f"bank{g}") for g, heads in enumerate(GROUPS)]
-        for bank, heads in zip(banks, GROUPS):
-            nc.tensor.matmul(bank[:].rearrange("p s i j -> p (s i j)"), zeros_bf[:, 0:P],
-                             zeros_bf[:, 0 : 2 * len(heads) * TOKENS], start=True, stop=True)
+
+        wk_swap = held.tile([P, HEADS, KB, P], BF16, name="wk_swap")
+        nc.vector.memset(wk_swap[:, :, :, 2 * HALF : P], 0.0)
 
         offsets = held.tile([P, TOKENS // 16], U16, name="offsets")
         y_sb = held.tile([P, KB, TOKENS], BF16, name="y_sb")
@@ -41,18 +39,24 @@ def tile_crossattention_s_kernel(tc, base, y, wk, rope_cos, rope_sin, offs, out)
             queue.dma_start(windows[h][:], base[h * P : (h + 1) * P, :])
 
         nc.sync.dma_start(y_sb[:], y.rearrange("(p kb) j -> p kb j", kb=KB))
-        load_wk(nc.scalar, 0)
+        load_wk(nc.sync, 0)
         nc.sync.dma_start(table[0:HALF, 1, :], rope_sin)
-        nc.scalar.dma_start(table[HALF : 2 * HALF, 1, :], rope_sin)
+        nc.sync.dma_start(table[HALF : 2 * HALF, 1, :], rope_sin)
         nc.sync.dma_start(table[0:HALF, 0, :], rope_cos)
-        nc.scalar.dma_start(table[HALF : 2 * HALF, 0, :], rope_cos)
+        nc.sync.dma_start(table[HALF : 2 * HALF, 0, :], rope_cos)
         nc.sync.dma_start(offsets[:], offs)
-        load_window(nc.scalar, 0)
+        load_window(nc.sync, 0)
         for pair in range(1, HEADS // 2):
             load_wk(nc.sync, pair)
-            load_window(nc.scalar, pair)
+            load_window(nc.sync, pair)
         for h in range(HEADS // 2, HEADS):
-            load_window(nc.sync if h % 2 == 0 else nc.scalar, h)
+            load_window(nc.sync, h)
+
+        for pair in range(HEADS // 2):
+            by_head = wk_sb[pair][:].rearrange("p kb (i c) -> p i kb c", i=2)
+            swapped = wk_swap[:, 2 * pair : 2 * pair + 2, :, :]
+            nc.scalar.copy(swapped[:, :, :, 0:HALF], by_head[:, :, :, HALF : 2 * HALF])
+            nc.scalar.copy(swapped[:, :, :, HALF : 2 * HALF], by_head[:, :, :, 0:HALF])
 
         nc.vector.tensor_scalar_mul(table[0:HALF, 1, :], table[0:HALF, 1, :], -1.0)
         nc.gpsimd.memset(table[2 * HALF : P, 0, :], 1.0)
@@ -67,10 +71,8 @@ def tile_crossattention_s_kernel(tc, base, y, wk, rope_cos, rope_sin, offs, out)
                     nc.tensor.matmul(bank[:, 0, i, :], wk_pair[:, kb, c0 : c0 + P], y_sb[:, kb, :],
                                      start=(kb == 0), stop=(kb == KB - 1))
                 for kb in range(KB):
-                    nc.tensor.matmul(bank[0:HALF, 1, i, :], wk_pair[:, kb, c0 + HALF : c0 + 2 * HALF],
-                                     y_sb[:, kb, :], start=(kb == 0), stop=(kb == KB - 1))
-                    nc.tensor.matmul(bank[HALF : 2 * HALF, 1, i, :], wk_pair[:, kb, c0 : c0 + HALF],
-                                     y_sb[:, kb, :], start=(kb == 0), stop=(kb == KB - 1))
+                    nc.tensor.matmul(bank[:, 1, i, :], wk_swap[:, h, kb, :], y_sb[:, kb, :],
+                                     start=(kb == 0), stop=(kb == KB - 1))
 
             ab = held.tile([P, 2, len(heads), TOKENS], F32, name=f"ab{g}")
             nc.vector.tensor_tensor(ab[:], bank[:], table[:].unsqueeze(2).to_broadcast([P, 2, len(heads), TOKENS]), MULT)

@@ -8,7 +8,7 @@ TOKENS = 128
 SLOTS = 256
 KB = 4
 HALF = 32
-GROUPS = ((0,), (1,), (2, 3), (4, 5), (6,), (7,))
+GROUPS = ((0,), (1,), (2,), (3,), (4, 5), (6, 7))
 
 BF16, F32, U16 = mybir.dt.bfloat16, mybir.dt.float32, mybir.dt.uint16
 MULT, ADD = mybir.AluOpType.mult, mybir.AluOpType.add
@@ -55,8 +55,9 @@ def tile_crossattention_s_kernel(tc, base, y, wk, rope_cos, rope_sin, offs, out)
         for pair in range(HEADS // 2):
             by_head = wk_sb[pair][:].rearrange("p kb (i c) -> p i kb c", i=2)
             swapped = wk_swap[:, 2 * pair : 2 * pair + 2, :, :]
-            nc.scalar.copy(swapped[:, :, :, 0:HALF], by_head[:, :, :, HALF : 2 * HALF])
-            nc.scalar.copy(swapped[:, :, :, HALF : 2 * HALF], by_head[:, :, :, 0:HALF])
+            copy = nc.vector.tensor_copy if pair == 0 else nc.scalar.copy
+            copy(swapped[:, :, :, 0:HALF], by_head[:, :, :, HALF : 2 * HALF])
+            copy(swapped[:, :, :, HALF : 2 * HALF], by_head[:, :, :, 0:HALF])
 
         nc.vector.tensor_scalar_mul(table[0:HALF, 1, :], table[0:HALF, 1, :], -1.0)
         nc.gpsimd.memset(table[2 * HALF : P, 0, :], 1.0)
@@ -78,4 +79,4 @@ def tile_crossattention_s_kernel(tc, base, y, wk, rope_cos, rope_sin, offs, out)
             nc.vector.tensor_tensor(ab[:], bank[:], table[:].unsqueeze(2).to_broadcast([P, 2, len(heads), TOKENS]), MULT)
             for i, h in enumerate(heads):
                 nc.vector.tensor_tensor(windows[h][:].indirect(offsets[:]), ab[:, 0, i, :], ab[:, 1, i, :], ADD)
-                (nc.sync if h % 2 == 0 else nc.scalar).dma_start(out[h * P : (h + 1) * P, :], windows[h][:])
+                nc.sync.dma_start(out[h * P : (h + 1) * P, :], windows[h][:])

@@ -18,10 +18,8 @@ def tile_crossattention_s_kernel(tc, base, y, wk, rope_cos, rope_sin, offs, out)
     nc = tc.nc
     with (
         tc.tile_pool(name="held", bufs=1) as held,
-        tc.psum_pool(name="psum", bufs=1) as psum,
+        tc.psum_pool(name="psum", bufs=4) as psum,
     ):
-        banks = [psum.tile([P, 2, len(heads), TOKENS], F32, name=f"bank{g}") for g, heads in enumerate(GROUPS)]
-
         wk_swap = held.tile([P, HEADS, KB, P], BF16, name="wk_swap")
         nc.vector.memset(wk_swap[:, :, :, 2 * HALF : P], 0.0)
 
@@ -64,19 +62,29 @@ def tile_crossattention_s_kernel(tc, base, y, wk, rope_cos, rope_sin, offs, out)
         nc.gpsimd.memset(table[2 * HALF : P, 1, :], 0.0)
 
         for g, heads in enumerate(GROUPS):
-            bank = banks[g]
+            for_heads = [P, len(heads), TOKENS]
+            k_ps = psum.tile(for_heads, F32, name="k_ps")
+            partner_ps = psum.tile(for_heads, F32, name="partner_ps")
             for i, h in enumerate(heads):
                 wk_pair = wk_sb[h // 2]
                 c0 = (h % 2) * P
                 for kb in range(KB):
-                    nc.tensor.matmul(bank[:, 0, i, :], wk_pair[:, kb, c0 : c0 + P], y_sb[:, kb, :],
+                    nc.tensor.matmul(k_ps[:, i, :], wk_pair[:, kb, c0 : c0 + P], y_sb[:, kb, :],
                                      start=(kb == 0), stop=(kb == KB - 1))
                 for kb in range(KB):
-                    nc.tensor.matmul(bank[:, 1, i, :], wk_swap[:, h, kb, :], y_sb[:, kb, :],
+                    nc.tensor.matmul(partner_ps[:, i, :], wk_swap[:, h, kb, :], y_sb[:, kb, :],
                                      start=(kb == 0), stop=(kb == KB - 1))
 
             ab = held.tile([P, 2, len(heads), TOKENS], F32, name=f"ab{g}")
-            nc.vector.tensor_tensor(ab[:], bank[:], table[:].unsqueeze(2).to_broadcast([P, 2, len(heads), TOKENS]), MULT)
+            cosines = table[:, 0:1, :].to_broadcast(for_heads)
+            sines = table[:, 1:2, :].to_broadcast(for_heads)
+            nc.vector.tensor_tensor(ab[:, 0], k_ps[:], cosines, MULT)
+            if g == 0:
+                nc.vector.tensor_tensor(ab[:, 1], partner_ps[:], sines, MULT)
+            else:
+                partner = held.tile(for_heads, F32, name=f"partner{g}")
+                nc.scalar.copy(partner[:], partner_ps[:])
+                nc.gpsimd.tensor_tensor(ab[:, 1], partner[:], sines, MULT)
             for i, h in enumerate(heads):
                 nc.vector.tensor_tensor(windows[h][:].indirect(offsets[:]), ab[:, 0, i, :], ab[:, 1, i, :], ADD)
                 nc.sync.dma_start(out[h * P : (h + 1) * P, :], windows[h][:])

@@ -8,6 +8,7 @@ TOKENS = 128
 SLOTS = 256
 KB = 4
 HALF = 32
+WARM_MATMULS = 8
 GROUPS = ((0,), (1,), (2,), (3,), (4, 5), (6, 7))
 
 BF16, F32, U16 = mybir.dt.bfloat16, mybir.dt.float32, mybir.dt.uint16
@@ -20,6 +21,12 @@ def tile_crossattention_s_kernel(tc, base, y, wk, rope_cos, rope_sin, offs, out)
         tc.tile_pool(name="held", bufs=1) as held,
         tc.psum_pool(name="psum", bufs=4) as psum,
     ):
+        zeros_bf = held.tile([P, 2 * TOKENS], BF16, name="zeros_bf")
+        nc.vector.memset(zeros_bf[:], 0.0)
+        for n in range(WARM_MATMULS):
+            warm_ps = psum.tile([P, 2 * TOKENS], F32, name="k_ps" if n % 2 == 0 else "partner_ps")
+            nc.tensor.matmul(warm_ps[:], zeros_bf[:, 0:P], zeros_bf[:], start=True, stop=True)
+
         wk_swap = held.tile([P, HEADS, KB, P], BF16, name="wk_swap")
         nc.vector.memset(wk_swap[:, :, :, 2 * HALF : P], 0.0)
 

@@ -8,7 +8,7 @@ TOKENS = 128
 SLOTS = 256
 KB = 4
 HALF = 32
-WARM_MATMULS = 8
+WARM_MATMULS = 10
 GROUPS = ((0,), (1,), (2,), (3,), (4, 5), (6, 7))
 
 BF16, F32, U16 = mybir.dt.bfloat16, mybir.dt.float32, mybir.dt.uint16
@@ -22,7 +22,7 @@ def tile_crossattention_s_kernel(tc, base, y, wk, rope_cos, rope_sin, offs, out)
         tc.psum_pool(name="psum", bufs=4) as psum,
     ):
         zeros_bf = held.tile([P, 2 * TOKENS], BF16, name="zeros_bf")
-        nc.vector.memset(zeros_bf[:], 0.0)
+        nc.gpsimd.memset(zeros_bf[:], 0.0)
         for n in range(WARM_MATMULS):
             warm_ps = psum.tile([P, 2 * TOKENS], F32, name="k_ps" if n % 2 == 0 else "partner_ps")
             nc.tensor.matmul(warm_ps[:], zeros_bf[:, 0:P], zeros_bf[:], start=True, stop=True)

@@ -1,15 +1,19 @@
 import concourse.mybir as mybir
+from concourse.masks import make_identity
 
 FLOPS = 2 * 512 * 1024 * 128
 
 P = 128
 HEADS = 8
+PAIRS = 4
 TOKENS = 128
 SLOTS = 256
 KB = 4
 HALF = 32
-WARM_MATMULS = 10
-GROUPS = ((0,), (1,), (2,), (3,), (4, 5), (6, 7))
+ROT = 2 * HALF
+WARM_MATMULS = 8
+GROUPS = ((0,), (1,), (2, 3), (4, 5), (6, 7))
+ON_VECTOR = 3
 
 BF16, F32, U16 = mybir.dt.bfloat16, mybir.dt.float32, mybir.dt.uint16
 MULT, ADD = mybir.AluOpType.mult, mybir.AluOpType.add
@@ -19,79 +23,95 @@ def tile_crossattention_s_kernel(tc, base, y, wk, rope_cos, rope_sin, offs, out)
     nc = tc.nc
     with (
         tc.tile_pool(name="held", bufs=1) as held,
-        tc.psum_pool(name="psum", bufs=4) as psum,
+        tc.psum_pool(name="psum_k", bufs=3) as psum_k,
+        tc.psum_pool(name="psum_ab", bufs=4) as psum_ab,
     ):
         zeros_bf = held.tile([P, 2 * TOKENS], BF16, name="zeros_bf")
         nc.gpsimd.memset(zeros_bf[:], 0.0)
         for n in range(WARM_MATMULS):
-            warm_ps = psum.tile([P, 2 * TOKENS], F32, name="k_ps" if n % 2 == 0 else "partner_ps")
+            warm_ps = psum_ab.tile([P, 2 * TOKENS], F32, name="ab_ps")
             nc.tensor.matmul(warm_ps[:], zeros_bf[:, 0:P], zeros_bf[:], start=True, stop=True)
 
-        wk_swap = held.tile([P, HEADS, KB, P], BF16, name="wk_swap")
-        nc.vector.memset(wk_swap[:, :, :, 2 * HALF : P], 0.0)
+        identity = held.tile([P, P], F32, name="identity")
+        make_identity(nc, identity[:])
 
         offsets = held.tile([P, TOKENS // 16], U16, name="offsets")
         y_sb = held.tile([P, KB, TOKENS], BF16, name="y_sb")
-        wk_sb = [held.tile([P, KB, 2 * P], BF16, name=f"wk_pair{pair}") for pair in range(HEADS // 2)]
+        wk_sb = [held.tile([P, KB, 2 * P], BF16, name=f"wk_pair{pair}") for pair in range(PAIRS)]
         wk_view = wk.rearrange("(p kb) c -> p kb c", kb=KB)
-        table = held.tile([P, 2, TOKENS], F32, name="table")
+        rope_rows = held.tile([ROT, TOKENS], F32, name="rope_rows")
         windows = [held.tile([P, SLOTS], F32, name=f"window{h}") for h in range(HEADS)]
 
-        def load_wk(queue, pair):
-            queue.dma_start(wk_sb[pair][:], wk_view[:, :, pair * 2 * P : (pair + 1) * 2 * P])
-
-        def load_window(queue, h):
-            queue.dma_start(windows[h][:], base[h * P : (h + 1) * P, :])
-
         nc.sync.dma_start(y_sb[:], y.rearrange("(p kb) j -> p kb j", kb=KB))
-        load_wk(nc.sync, 0)
-        nc.sync.dma_start(table[0:HALF, 1, :], rope_sin)
-        nc.sync.dma_start(table[HALF : 2 * HALF, 1, :], rope_sin)
-        nc.sync.dma_start(table[0:HALF, 0, :], rope_cos)
-        nc.sync.dma_start(table[HALF : 2 * HALF, 0, :], rope_cos)
+        nc.sync.dma_start(wk_sb[0][:], wk_view[:, :, 0 : 2 * P])
+        nc.sync.dma_start(rope_rows[0:HALF, :], rope_cos)
+        nc.sync.dma_start(rope_rows[HALF:ROT, :], rope_sin)
         nc.sync.dma_start(offsets[:], offs)
-        load_window(nc.sync, 0)
-        for pair in range(1, HEADS // 2):
-            load_wk(nc.sync, pair)
-            load_window(nc.sync, pair)
-        for h in range(HEADS // 2, HEADS):
-            load_window(nc.sync, h)
+        nc.sync.dma_start(windows[0][:], base[0:P, :])
+        for pair in range(1, PAIRS):
+            nc.sync.dma_start(wk_sb[pair][:], wk_view[:, :, pair * 2 * P : (pair + 1) * 2 * P])
+            nc.sync.dma_start(windows[pair][:], base[pair * P : (pair + 1) * P, :])
+        for h in range(PAIRS, HEADS):
+            nc.sync.dma_start(windows[h][:], base[h * P : (h + 1) * P, :])
 
-        for pair in range(HEADS // 2):
-            by_head = wk_sb[pair][:].rearrange("p kb (i c) -> p i kb c", i=2)
-            swapped = wk_swap[:, 2 * pair : 2 * pair + 2, :, :]
-            copy = nc.vector.tensor_copy if pair == 0 else nc.scalar.copy
-            copy(swapped[:, :, :, 0:HALF], by_head[:, :, :, HALF : 2 * HALF])
-            copy(swapped[:, :, :, HALF : 2 * HALF], by_head[:, :, :, 0:HALF])
+        rope_ps = psum_k.tile([P, ROT], F32, name="k_tok_ps")
+        nc.tensor.transpose(rope_ps[:], rope_rows[:], identity[0:ROT, 0:ROT])
+        factor_a = held.tile([P, 1, P], F32, name="factor_a")
+        factor_b = held.tile([P, 1, ROT], F32, name="factor_b")
+        nc.vector.memset(factor_a[:, :, ROT:P], 1.0)
+        nc.vector.tensor_copy(factor_a[:, 0, 0:HALF], rope_ps[:, 0:HALF])
+        nc.vector.tensor_copy(factor_a[:, 0, HALF:ROT], rope_ps[:, 0:HALF])
+        nc.vector.tensor_scalar_mul(factor_b[:, 0, 0:HALF], rope_ps[:, HALF:ROT], -1.0)
+        nc.vector.tensor_copy(factor_b[:, 0, HALF:ROT], rope_ps[:, HALF:ROT])
 
-        nc.vector.tensor_scalar_mul(table[0:HALF, 1, :], table[0:HALF, 1, :], -1.0)
-        nc.gpsimd.memset(table[2 * HALF : P, 0, :], 1.0)
-        nc.gpsimd.memset(table[2 * HALF : P, 1, :], 0.0)
+        a_tok = held.tile([P, HEADS, P], F32, name="a_tok")
+        b_tok = held.tile([P, HEADS, P], F32, name="b_tok")
+        nc.vector.memset(b_tok[:, :, ROT:P], 0.0)
+        k_tok_ps = {}
 
-        for g, heads in enumerate(GROUPS):
-            for_heads = [P, len(heads), TOKENS]
-            k_ps = psum.tile(for_heads, F32, name="k_ps")
-            partner_ps = psum.tile(for_heads, F32, name="partner_ps")
-            for i, h in enumerate(heads):
-                wk_pair = wk_sb[h // 2]
-                c0 = (h % 2) * P
-                for kb in range(KB):
-                    nc.tensor.matmul(k_ps[:, i, :], wk_pair[:, kb, c0 : c0 + P], y_sb[:, kb, :],
-                                     start=(kb == 0), stop=(kb == KB - 1))
-                for kb in range(KB):
-                    nc.tensor.matmul(partner_ps[:, i, :], wk_swap[:, h, kb, :], y_sb[:, kb, :],
-                                     start=(kb == 0), stop=(kb == KB - 1))
+        def project(g):
+            first, n = GROUPS[g][0], len(GROUPS[g])
+            c0 = (first % 2) * P
+            k_tok_ps[g] = psum_k.tile([P, n, P], F32, name="k_tok_ps")
+            for kb in range(KB):
+                nc.tensor.matmul(k_tok_ps[g][:].rearrange("p i c -> p (i c)"), y_sb[:, kb, :],
+                                 wk_sb[first // 2][:, kb, c0 : c0 + n * P], start=(kb == 0), stop=(kb == KB - 1))
 
-            ab = held.tile([P, 2, len(heads), TOKENS], F32, name=f"ab{g}")
-            cosines = table[:, 0:1, :].to_broadcast(for_heads)
-            sines = table[:, 1:2, :].to_broadcast(for_heads)
-            nc.vector.tensor_tensor(ab[:, 0], k_ps[:], cosines, MULT)
-            if g == 0:
-                nc.vector.tensor_tensor(ab[:, 1], partner_ps[:], sines, MULT)
+        def rotate(g):
+            first, n = GROUPS[g][0], len(GROUPS[g])
+            a_group = a_tok[:, first : first + n, :]
+            b_group = b_tok[:, first : first + n, :]
+            if g < ON_VECTOR:
+                engine, k_read = nc.vector, k_tok_ps[g][:]
+                nc.vector.tensor_tensor(a_group, k_read, factor_a[:].to_broadcast([P, n, P]), MULT)
             else:
-                partner = held.tile(for_heads, F32, name=f"partner{g}")
-                nc.scalar.copy(partner[:], partner_ps[:])
-                nc.gpsimd.tensor_tensor(ab[:, 1], partner[:], sines, MULT)
-            for i, h in enumerate(heads):
-                nc.vector.tensor_tensor(windows[h][:].indirect(offsets[:]), ab[:, 0, i, :], ab[:, 1, i, :], ADD)
-                nc.sync.dma_start(out[h * P : (h + 1) * P, :], windows[h][:])
+                engine, k_read = nc.gpsimd, a_group
+                nc.scalar.copy(a_group, k_tok_ps[g][:])
+            engine.tensor_tensor(b_group[:, :, 0:HALF], k_read[:, :, HALF:ROT],
+                                 factor_b[:, :, 0:HALF].to_broadcast([P, n, HALF]), MULT)
+            engine.tensor_tensor(b_group[:, :, HALF:ROT], k_read[:, :, 0:HALF],
+                                 factor_b[:, :, HALF:ROT].to_broadcast([P, n, HALF]), MULT)
+            if g >= ON_VECTOR:
+                engine.tensor_tensor(a_group[:, :, 0:ROT], a_group[:, :, 0:ROT],
+                                     factor_a[:, :, 0:ROT].to_broadcast([P, n, ROT]), MULT)
+
+        def place(h):
+            ab_ps = psum_ab.tile([P, 2, TOKENS], F32, name="ab_ps")
+            nc.tensor.transpose(ab_ps[:, 0, :], a_tok[:, h, :], identity[:])
+            nc.tensor.transpose(ab_ps[:, 1, :], b_tok[:, h, :], identity[:])
+            ab = held.tile([P, 2, TOKENS], F32, name=f"ab{h}")
+            nc.scalar.copy(ab[:], ab_ps[:])
+            nc.vector.tensor_tensor(windows[h][:].indirect(offsets[:]), ab[:, 0, :], ab[:, 1, :], ADD)
+            nc.sync.dma_start(out[h * P : (h + 1) * P, :], windows[h][:])
+
+        project(0)
+        project(1)
+        project(2)
+        rotate(0)
+        for g in range(len(GROUPS)):
+            if g + 1 < len(GROUPS):
+                rotate(g + 1)
+            for h in GROUPS[g]:
+                place(h)
+            if g + 3 < len(GROUPS):
+                project(g + 3)

@@ -13,7 +13,6 @@ HALF = 32
 ROT = 2 * HALF
 WARM_MATMULS = 8
 GROUPS = ((0,), (1,), (2, 3), (4, 5), (6, 7))
-ON_VECTOR = 3
 
 BF16, F32, U16 = mybir.dt.bfloat16, mybir.dt.float32, mybir.dt.uint16
 MULT, ADD = mybir.AluOpType.mult, mybir.AluOpType.add
@@ -42,32 +41,41 @@ def tile_crossattention_s_kernel(tc, base, y, wk, rope_cos, rope_sin, offs, out)
         rope_rows = held.tile([ROT, TOKENS], F32, name="rope_rows")
         windows = [held.tile([P, SLOTS], F32, name=f"window{h}") for h in range(HEADS)]
 
+        def load_wk(pair):
+            nc.sync.dma_start(wk_sb[pair][:], wk_view[:, :, pair * 2 * P : (pair + 1) * 2 * P])
+
+        def load_window(h):
+            nc.sync.dma_start(windows[h][:], base[h * P : (h + 1) * P, :])
+
         nc.sync.dma_start(y_sb[:], y.rearrange("(p kb) j -> p kb j", kb=KB))
-        nc.sync.dma_start(wk_sb[0][:], wk_view[:, :, 0 : 2 * P])
+        load_wk(0)
         nc.sync.dma_start(rope_rows[0:HALF, :], rope_cos)
         nc.sync.dma_start(rope_rows[HALF:ROT, :], rope_sin)
+        load_wk(1)
         nc.sync.dma_start(offsets[:], offs)
-        nc.sync.dma_start(windows[0][:], base[0:P, :])
-        for pair in range(1, PAIRS):
-            nc.sync.dma_start(wk_sb[pair][:], wk_view[:, :, pair * 2 * P : (pair + 1) * 2 * P])
-            nc.sync.dma_start(windows[pair][:], base[pair * P : (pair + 1) * P, :])
-        for h in range(PAIRS, HEADS):
-            nc.sync.dma_start(windows[h][:], base[h * P : (h + 1) * P, :])
+        load_window(0)
+        load_wk(2)
+        load_wk(3)
+        for h in range(1, HEADS):
+            load_window(h)
 
         rope_ps = psum_k.tile([P, ROT], F32, name="k_tok_ps")
         nc.tensor.transpose(rope_ps[:], rope_rows[:], identity[0:ROT, 0:ROT])
-        factor_a = held.tile([P, 1, P], F32, name="factor_a")
-        factor_b = held.tile([P, 1, ROT], F32, name="factor_b")
-        nc.vector.memset(factor_a[:, :, ROT:P], 1.0)
-        nc.vector.tensor_copy(factor_a[:, 0, 0:HALF], rope_ps[:, 0:HALF])
-        nc.vector.tensor_copy(factor_a[:, 0, HALF:ROT], rope_ps[:, 0:HALF])
-        nc.vector.tensor_scalar_mul(factor_b[:, 0, 0:HALF], rope_ps[:, HALF:ROT], -1.0)
-        nc.vector.tensor_copy(factor_b[:, 0, HALF:ROT], rope_ps[:, HALF:ROT])
+        factor_a = held.tile([P, 1, 2, HALF], F32, name="factor_a")
+        factor_b = held.tile([P, 1, 2, HALF], F32, name="factor_b")
+        nc.vector.tensor_copy(factor_a[:, 0, 0, :], rope_ps[:, 0:HALF])
+        nc.vector.tensor_copy(factor_a[:, 0, 1, :], rope_ps[:, 0:HALF])
+        nc.vector.tensor_scalar_mul(factor_b[:, 0, 0, :], rope_ps[:, HALF:ROT], -1.0)
+        nc.vector.tensor_copy(factor_b[:, 0, 1, :], rope_ps[:, HALF:ROT])
 
         a_tok = held.tile([P, HEADS, P], F32, name="a_tok")
         b_tok = held.tile([P, HEADS, P], F32, name="b_tok")
         nc.vector.memset(b_tok[:, :, ROT:P], 0.0)
         k_tok_ps = {}
+        ab = {}
+
+        def halves(rotated):
+            return rotated.rearrange("p i (x f) -> p i x f", x=2)
 
         def project(g):
             first, n = GROUPS[g][0], len(GROUPS[g])
@@ -79,39 +87,37 @@ def tile_crossattention_s_kernel(tc, base, y, wk, rope_cos, rope_sin, offs, out)
 
         def rotate(g):
             first, n = GROUPS[g][0], len(GROUPS[g])
+            k_ps = k_tok_ps[g][:]
             a_group = a_tok[:, first : first + n, :]
             b_group = b_tok[:, first : first + n, :]
-            if g < ON_VECTOR:
-                engine, k_read = nc.vector, k_tok_ps[g][:]
-                nc.vector.tensor_tensor(a_group, k_read, factor_a[:].to_broadcast([P, n, P]), MULT)
-            else:
-                engine, k_read = nc.gpsimd, a_group
-                nc.scalar.copy(a_group, k_tok_ps[g][:])
-            engine.tensor_tensor(b_group[:, :, 0:HALF], k_read[:, :, HALF:ROT],
-                                 factor_b[:, :, 0:HALF].to_broadcast([P, n, HALF]), MULT)
-            engine.tensor_tensor(b_group[:, :, HALF:ROT], k_read[:, :, 0:HALF],
-                                 factor_b[:, :, HALF:ROT].to_broadcast([P, n, HALF]), MULT)
-            if g >= ON_VECTOR:
-                engine.tensor_tensor(a_group[:, :, 0:ROT], a_group[:, :, 0:ROT],
-                                     factor_a[:, :, 0:ROT].to_broadcast([P, n, ROT]), MULT)
+            nc.vector.tensor_tensor(halves(a_group[:, :, 0:ROT]), halves(k_ps[:, :, 0:ROT]),
+                                    factor_a[:].to_broadcast([P, n, 2, HALF]), MULT)
+            nc.vector.tensor_tensor(halves(b_group[:, :, 0:ROT]), halves(k_ps[:, :, 0:ROT])[:, :, ::-1, :],
+                                    factor_b[:].to_broadcast([P, n, 2, HALF]), MULT)
+            nc.scalar.copy(a_group[:, :, ROT:P], k_ps[:, :, ROT:P])
 
-        def place(h):
-            ab_ps = psum_ab.tile([P, 2, TOKENS], F32, name="ab_ps")
-            nc.tensor.transpose(ab_ps[:, 0, :], a_tok[:, h, :], identity[:])
-            nc.tensor.transpose(ab_ps[:, 1, :], b_tok[:, h, :], identity[:])
-            ab = held.tile([P, 2, TOKENS], F32, name=f"ab{h}")
-            nc.scalar.copy(ab[:], ab_ps[:])
-            nc.vector.tensor_tensor(windows[h][:].indirect(offsets[:]), ab[:, 0, :], ab[:, 1, :], ADD)
-            nc.sync.dma_start(out[h * P : (h + 1) * P, :], windows[h][:])
+        def turn(g):
+            for h in GROUPS[g]:
+                ab_ps = psum_ab.tile([P, 2, TOKENS], F32, name="ab_ps")
+                nc.tensor.transpose(ab_ps[:, 0, :], a_tok[:, h, :], identity[:])
+                nc.tensor.transpose(ab_ps[:, 1, :], b_tok[:, h, :], identity[:])
+                ab[h] = held.tile([P, 2, TOKENS], F32, name=f"ab{h}")
+                nc.scalar.copy(ab[h][:], ab_ps[:])
 
+        def place(g):
+            for h in GROUPS[g]:
+                nc.vector.tensor_tensor(windows[h][:].indirect(offsets[:]), ab[h][:, 0, :], ab[h][:, 1, :], ADD)
+                nc.sync.dma_start(out[h * P : (h + 1) * P, :], windows[h][:])
+
+        steps = len(GROUPS)
         project(0)
         project(1)
-        project(2)
-        rotate(0)
-        for g in range(len(GROUPS)):
-            if g + 1 < len(GROUPS):
-                rotate(g + 1)
-            for h in GROUPS[g]:
-                place(h)
-            if g + 3 < len(GROUPS):
-                project(g + 3)
+        for s in range(steps + 2):
+            if s < steps:
+                rotate(s)
+            if 0 <= s - 1 < steps:
+                turn(s - 1)
+            if 0 <= s - 2 < steps:
+                place(s - 2)
+            if s + 2 < steps:
+                project(s + 2)

@@ -22,13 +22,12 @@ def tile_crossattention_s_kernel(tc, base, y, wk, rope_cos, rope_sin, offs, out)
     nc = tc.nc
     with (
         tc.tile_pool(name="held", bufs=1) as held,
-        tc.psum_pool(name="psum_k", bufs=3) as psum_k,
-        tc.psum_pool(name="psum_ab", bufs=4) as psum_ab,
+        tc.psum_pool(name="psum", bufs=8) as psum,
     ):
         zeros_bf = held.tile([P, 2 * TOKENS], BF16, name="zeros_bf")
         nc.gpsimd.memset(zeros_bf[:], 0.0)
         for n in range(WARM_MATMULS):
-            warm_ps = psum_ab.tile([P, 2 * TOKENS], F32, name="ab_ps")
+            warm_ps = psum.tile([P, 2 * TOKENS], F32, name="bank")
             nc.tensor.matmul(warm_ps[:], zeros_bf[:, 0:P], zeros_bf[:], start=True, stop=True)
 
         identity = held.tile([P, P], F32, name="identity")
@@ -47,10 +46,10 @@ def tile_crossattention_s_kernel(tc, base, y, wk, rope_cos, rope_sin, offs, out)
         def load_window(h):
             nc.sync.dma_start(windows[h][:], base[h * P : (h + 1) * P, :])
 
-        nc.sync.dma_start(y_sb[:], y.rearrange("(p kb) j -> p kb j", kb=KB))
-        load_wk(0)
         nc.sync.dma_start(rope_rows[0:HALF, :], rope_cos)
         nc.sync.dma_start(rope_rows[HALF:ROT, :], rope_sin)
+        nc.sync.dma_start(y_sb[:], y.rearrange("(p kb) j -> p kb j", kb=KB))
+        load_wk(0)
         load_wk(1)
         nc.sync.dma_start(offsets[:], offs)
         load_window(0)
@@ -59,7 +58,7 @@ def tile_crossattention_s_kernel(tc, base, y, wk, rope_cos, rope_sin, offs, out)
         for h in range(1, HEADS):
             load_window(h)
 
-        rope_ps = psum_k.tile([P, ROT], F32, name="k_tok_ps")
+        rope_ps = psum.tile([P, ROT], F32, name="bank")
         nc.tensor.transpose(rope_ps[:], rope_rows[:], identity[0:ROT, 0:ROT])
         factor_a = held.tile([P, 1, 2, HALF], F32, name="factor_a")
         factor_b = held.tile([P, 1, 2, HALF], F32, name="factor_b")
@@ -71,7 +70,8 @@ def tile_crossattention_s_kernel(tc, base, y, wk, rope_cos, rope_sin, offs, out)
         a_tok = held.tile([P, HEADS, P], F32, name="a_tok")
         b_tok = held.tile([P, HEADS, P], F32, name="b_tok")
         nc.vector.memset(b_tok[:, :, ROT:P], 0.0)
-        k_tok_ps = {}
+        rot_ps = {}
+        plain_ps = {}
         ab = {}
 
         def halves(rotated):
@@ -79,26 +79,30 @@ def tile_crossattention_s_kernel(tc, base, y, wk, rope_cos, rope_sin, offs, out)
 
         def project(g):
             first, n = GROUPS[g][0], len(GROUPS[g])
-            c0 = (first % 2) * P
-            k_tok_ps[g] = psum_k.tile([P, n, P], F32, name="k_tok_ps")
+            i0 = first % 2
+            by_head = wk_sb[first // 2][:].rearrange("p kb (i c) -> p kb i c", i=2)
+            rot_ps[g] = psum.tile([P, n, ROT], F32, name="bank")
             for kb in range(KB):
-                nc.tensor.matmul(k_tok_ps[g][:].rearrange("p i c -> p (i c)"), y_sb[:, kb, :],
-                                 wk_sb[first // 2][:, kb, c0 : c0 + n * P], start=(kb == 0), stop=(kb == KB - 1))
+                nc.tensor.matmul(rot_ps[g][:], y_sb[:, kb, :], by_head[:, kb, i0 : i0 + n, 0:ROT],
+                                 start=(kb == 0), stop=(kb == KB - 1))
+            plain_ps[g] = psum.tile([P, n, P - ROT], F32, name="bank")
+            for kb in range(KB):
+                nc.tensor.matmul(plain_ps[g][:], y_sb[:, kb, :], by_head[:, kb, i0 : i0 + n, ROT:P],
+                                 start=(kb == 0), stop=(kb == KB - 1))
 
         def rotate(g):
             first, n = GROUPS[g][0], len(GROUPS[g])
-            k_ps = k_tok_ps[g][:]
             a_group = a_tok[:, first : first + n, :]
             b_group = b_tok[:, first : first + n, :]
-            nc.vector.tensor_tensor(halves(a_group[:, :, 0:ROT]), halves(k_ps[:, :, 0:ROT]),
+            nc.vector.tensor_tensor(halves(a_group[:, :, 0:ROT]), halves(rot_ps[g][:]),
                                     factor_a[:].to_broadcast([P, n, 2, HALF]), MULT)
-            nc.vector.tensor_tensor(halves(b_group[:, :, 0:ROT]), halves(k_ps[:, :, 0:ROT])[:, :, ::-1, :],
+            nc.vector.tensor_tensor(halves(b_group[:, :, 0:ROT]), halves(rot_ps[g][:])[:, :, ::-1, :],
                                     factor_b[:].to_broadcast([P, n, 2, HALF]), MULT)
-            nc.scalar.copy(a_group[:, :, ROT:P], k_ps[:, :, ROT:P])
+            nc.scalar.copy(a_group[:, :, ROT:P], plain_ps[g][:])
 
         def turn(g):
             for h in GROUPS[g]:
-                ab_ps = psum_ab.tile([P, 2, TOKENS], F32, name="ab_ps")
+                ab_ps = psum.tile([P, 2, TOKENS], F32, name="bank")
                 nc.tensor.transpose(ab_ps[:, 0, :], a_tok[:, h, :], identity[:])
                 nc.tensor.transpose(ab_ps[:, 1, :], b_tok[:, h, :], identity[:])
                 ab[h] = held.tile([P, 2, TOKENS], F32, name=f"ab{h}")
@@ -110,8 +114,9 @@ def tile_crossattention_s_kernel(tc, base, y, wk, rope_cos, rope_sin, offs, out)
                 nc.sync.dma_start(out[h * P : (h + 1) * P, :], windows[h][:])
 
         steps = len(GROUPS)
-        project(0)
-        project(1)
+        AT_ONCE = 3
+        for g in range(AT_ONCE):
+            project(g)
         for s in range(steps + 2):
             if s < steps:
                 rotate(s)
@@ -119,5 +124,5 @@ def tile_crossattention_s_kernel(tc, base, y, wk, rope_cos, rope_sin, offs, out)
                 turn(s - 1)
             if 0 <= s - 2 < steps:
                 place(s - 2)
-            if s + 2 < steps:
-                project(s + 2)
+            if AT_ONCE <= s + 1 < steps:
+                project(s + 1)

@@ -114,7 +114,7 @@ def tile_crossattention_s_kernel(tc, base, y, wk, rope_cos, rope_sin, offs, out)
                 nc.sync.dma_start(out[h * P : (h + 1) * P, :], windows[h][:])
 
         steps = len(GROUPS)
-        AT_ONCE = 3
+        AT_ONCE = 2
         for g in range(AT_ONCE):
             project(g)
         for s in range(steps + 2):

@@ -11,7 +11,7 @@ SLOTS = 256
 KB = 4
 HALF = 32
 ROT = 2 * HALF
-WARM_MATMULS = 8
+WARM_MATMULS = 6
 GROUPS = ((0,), (1,), (2, 3), (4, 5), (6, 7))
 
 BF16, F32, U16 = mybir.dt.bfloat16, mybir.dt.float32, mybir.dt.uint16

import concourse.mybir as mybir
from concourse.masks import make_identity

FLOPS = 2 * 512 * 1024 * 128

P = 128
HEADS = 8
PAIRS = 4
TOKENS = 128
SLOTS = 256
KB = 4
HALF = 32
ROT = 2 * HALF
WARM_MATMULS = 6
GROUPS = ((0,), (1,), (2, 3), (4, 5), (6, 7))

BF16, F32, U16 = mybir.dt.bfloat16, mybir.dt.float32, mybir.dt.uint16
MULT, ADD = mybir.AluOpType.mult, mybir.AluOpType.add


def tile_crossattention_s_kernel(tc, base, y, wk, rope_cos, rope_sin, offs, out):
    nc = tc.nc
    with (
        tc.tile_pool(name="held", bufs=1) as held,
        tc.psum_pool(name="psum", bufs=8) as psum,
    ):
        zeros_bf = held.tile([P, 2 * TOKENS], BF16, name="zeros_bf")
        nc.gpsimd.memset(zeros_bf[:], 0.0)
        for n in range(WARM_MATMULS):
            warm_ps = psum.tile([P, 2 * TOKENS], F32, name="bank")
            nc.tensor.matmul(warm_ps[:], zeros_bf[:, 0:P], zeros_bf[:], start=True, stop=True)

        identity = held.tile([P, P], F32, name="identity")
        make_identity(nc, identity[:])

        offsets = held.tile([P, TOKENS // 16], U16, name="offsets")
        y_sb = held.tile([P, KB, TOKENS], BF16, name="y_sb")
        wk_sb = [held.tile([P, KB, 2 * P], BF16, name=f"wk_pair{pair}") for pair in range(PAIRS)]
        wk_view = wk.rearrange("(p kb) c -> p kb c", kb=KB)
        rope_rows = held.tile([ROT, TOKENS], F32, name="rope_rows")
        windows = [held.tile([P, SLOTS], F32, name=f"window{h}") for h in range(HEADS)]

        def load_wk(pair):
            nc.sync.dma_start(wk_sb[pair][:], wk_view[:, :, pair * 2 * P : (pair + 1) * 2 * P])

        def load_window(h):
            nc.sync.dma_start(windows[h][:], base[h * P : (h + 1) * P, :])

        nc.sync.dma_start(rope_rows[0:HALF, :], rope_cos)
        nc.sync.dma_start(rope_rows[HALF:ROT, :], rope_sin)
        nc.sync.dma_start(y_sb[:], y.rearrange("(p kb) j -> p kb j", kb=KB))
        load_wk(0)
        load_wk(1)
        nc.sync.dma_start(offsets[:], offs)
        load_window(0)
        load_wk(2)
        load_wk(3)
        for h in range(1, HEADS):
            load_window(h)

        rope_ps = psum.tile([P, ROT], F32, name="bank")
        nc.tensor.transpose(rope_ps[:], rope_rows[:], identity[0:ROT, 0:ROT])
        factor_a = held.tile([P, 1, 2, HALF], F32, name="factor_a")
        factor_b = held.tile([P, 1, 2, HALF], F32, name="factor_b")
        nc.vector.tensor_copy(factor_a[:, 0, 0, :], rope_ps[:, 0:HALF])
        nc.vector.tensor_copy(factor_a[:, 0, 1, :], rope_ps[:, 0:HALF])
        nc.vector.tensor_scalar_mul(factor_b[:, 0, 0, :], rope_ps[:, HALF:ROT], -1.0)
        nc.vector.tensor_copy(factor_b[:, 0, 1, :], rope_ps[:, HALF:ROT])

        a_tok = held.tile([P, HEADS, P], F32, name="a_tok")
        b_tok = held.tile([P, HEADS, P], F32, name="b_tok")
        nc.vector.memset(b_tok[:, :, ROT:P], 0.0)
        rot_ps = {}
        plain_ps = {}
        ab = {}

        def halves(rotated):
            return rotated.rearrange("p i (x f) -> p i x f", x=2)

        def project(g):
            first, n = GROUPS[g][0], len(GROUPS[g])
            i0 = first % 2
            by_head = wk_sb[first // 2][:].rearrange("p kb (i c) -> p kb i c", i=2)
            rot_ps[g] = psum.tile([P, n, ROT], F32, name="bank")
            for kb in range(KB):
                nc.tensor.matmul(rot_ps[g][:], y_sb[:, kb, :], by_head[:, kb, i0 : i0 + n, 0:ROT],
                                 start=(kb == 0), stop=(kb == KB - 1))
            plain_ps[g] = psum.tile([P, n, P - ROT], F32, name="bank")
            for kb in range(KB):
                nc.tensor.matmul(plain_ps[g][:], y_sb[:, kb, :], by_head[:, kb, i0 : i0 + n, ROT:P],
                                 start=(kb == 0), stop=(kb == KB - 1))

        def rotate(g):
            first, n = GROUPS[g][0], len(GROUPS[g])
            a_group = a_tok[:, first : first + n, :]
            b_group = b_tok[:, first : first + n, :]
            nc.vector.tensor_tensor(halves(a_group[:, :, 0:ROT]), halves(rot_ps[g][:]),
                                    factor_a[:].to_broadcast([P, n, 2, HALF]), MULT)
            nc.vector.tensor_tensor(halves(b_group[:, :, 0:ROT]), halves(rot_ps[g][:])[:, :, ::-1, :],
                                    factor_b[:].to_broadcast([P, n, 2, HALF]), MULT)
            nc.scalar.copy(a_group[:, :, ROT:P], plain_ps[g][:])

        def turn(g):
            for h in GROUPS[g]:
                ab_ps = psum.tile([P, 2, TOKENS], F32, name="bank")
                nc.tensor.transpose(ab_ps[:, 0, :], a_tok[:, h, :], identity[:])
                nc.tensor.transpose(ab_ps[:, 1, :], b_tok[:, h, :], identity[:])
                ab[h] = held.tile([P, 2, TOKENS], F32, name=f"ab{h}")
                nc.scalar.copy(ab[h][:], ab_ps[:])

        def place(g):
            for h in GROUPS[g]:
                nc.vector.tensor_tensor(windows[h][:].indirect(offsets[:]), ab[h][:, 0, :], ab[h][:, 1, :], ADD)
                nc.sync.dma_start(out[h * P : (h + 1) * P, :], windows[h][:])

        steps = len(GROUPS)
        AT_ONCE = 2
        for g in range(AT_ONCE):
            project(g)
        for s in range(steps + 2):
            if s < steps:
                rotate(s)
            if 0 <= s - 1 < steps:
                turn(s - 1)
            if 0 <= s - 2 < steps:
                place(s - 2)
            if AT_ONCE <= s + 1 < steps:
                project(s + 1)
